import numpy as np
import ml_dtypes


def mxq(x, axis, fmt="e4m3"):
    dtype, down = {"e4m3": (ml_dtypes.float8_e4m3fn, 7), "e5m2": (ml_dtypes.float8_e5m2, 14)}[fmt]
    v = np.moveaxis(np.asarray(x, np.float32).astype(ml_dtypes.bfloat16).astype(np.float64), axis, -1)
    blocks = v.reshape(v.shape[:-1] + (-1, 32))
    amax = np.abs(blocks).max(-1, keepdims=True)
    byte = np.maximum(np.where(amax > 0, np.frexp(amax)[1] - 1 + 127, 0) - down, 1)
    scale = np.exp2(byte - 127.0)
    codes = (blocks / scale).astype(np.float32).astype(dtype).astype(np.float64)
    return np.moveaxis((codes * scale).reshape(v.shape), -1, axis)


WIDE = False


def mx_kscale(k):
    if not WIDE:
        return np.ones(k)
    levels = np.array([10, -10, 5, -5, 0])
    a = np.random.permutation(np.resize(levels, k // 512 * 4)).reshape(k // 512, 4)
    idx = np.arange(k)
    return np.exp2(a[idx // 512, idx % 128 // 32])


BF16 = ml_dtypes.bfloat16


def bf(x):
    return np.asarray(x, np.float32).astype(BF16)


def f64(x):
    return np.asarray(x).astype(np.float64)


N, C, H, W, B = 1024, 8, 4, 4, 8192
D = C * H * W


def setup_inputs():
    s = mx_kscale(N)
    sig = (0.5 + 0.5 * np.random.random((B, 1))) * (1.0 + np.random.random((B, 1)))
    z = np.random.standard_normal((B, N)) * sig
    e = np.exp(z - z.max(1, keepdims=True))
    w = e / e.sum(1, keepdims=True)
    memory = np.random.standard_normal((N, D)) * (0.5 + np.random.random((N, 1))) * 3.0
    add = np.random.standard_normal((B, C, H, W)) * 3.0 * np.sqrt(N / B)
    return {"w": bf(w * s), "memory": bf((memory / s[:, None]).reshape(N, C, H, W)), "add": bf(add / np.mean(s * s))}


def reference(w, memory, add):
    wf = f64(w)
    mem_flat = f64(memory).reshape(N, D)
    a = f64(add).reshape(B, D)
    new_memory = mem_flat + wf.T @ a
    r = mxq(wf, 1, "e4m3") @ mxq(new_memory, 0, "e4m3")
    return r.reshape(B, C, H, W)

@@ -1,0 +1,233 @@
+from contextlib import ExitStack
+
+import concourse.mybir as mybir
+from concourse.masks import make_identity
+
+F32 = mybir.dt.float32
+BF16 = mybir.dt.bfloat16
+U32 = mybir.dt.uint32
+U8 = mybir.dt.uint8
+FP8X4 = mybir.dt.float8_e4m3fn_x4
+
+P = 128
+KEYS = 8192
+SLOTS = 1024
+D = 128
+CHUNKS = KEYS // P
+HALF = 512
+GROUP = 4
+GROUPS = CHUNKS // GROUP
+FLOPS = 2 * 2 * KEYS * SLOTS * D
+
+W_PLAN = [(0, 1), (1, 1), (2, 2)] + [(j, 4) for j in range(4, 60, 4)] + [(60, 1), (61, 1), (62, 1), (63, 1)]
+A_PLAN = [(0, 4), (4, 12), (16, 16), (32, 16), (48, 16)]
+W_BUFS = 8
+AHEAD = W_BUFS - 1
+MEM_AT = 6
+LATE = 4
+R_BANKS = [0, 1, 6, 7, 2, 3, 4, 5]
+R_ON_VECTOR = [0, 3, 5, 7, 9, 11, 13, 15]
+
+
+def tile_memory_pb_t_kernel(tc, w, memory, add, out):
+    nc = tc.nc
+    w_rows = w.rearrange("(p j) n -> p (j n)", j=CHUNKS)
+    a_rows = add.rearrange("(p j) c h w -> p (j c h w)", j=CHUNKS)
+    o_rows = out.rearrange("(p j) c h w -> p (j c h w)", j=CHUNKS)
+    m_rows = memory.rearrange("(c p) a h w -> p c (a h w)", p=P)
+
+    with ExitStack() as ctx:
+        const = ctx.enter_context(tc.tile_pool(name="const", bufs=1))
+        keep = ctx.enter_context(tc.tile_pool(name="keep", bufs=1))
+        wpool = ctx.enter_context(tc.tile_pool(name="wpool", bufs=W_BUFS))
+        gpool = ctx.enter_context(tc.tile_pool(name="gpool", bufs=3))
+        opool = ctx.enter_context(tc.tile_pool(name="opool", bufs=6))
+        psum = ctx.enter_context(tc.psum_pool(name="psum", bufs=1))
+        ctx.enter_context(tc.manual_schedule())
+
+        def bank(index, dtype):
+            return psum.tile([P, HALF], dtype, name="ps%d" % index, tag="b%d" % index)
+
+        ident_f = const.tile([P, P], F32, name="ident_f")
+        make_identity(nc, ident_f[:])
+        ident_b = const.tile([P, P], BF16, name="ident_b")
+        make_identity(nc, ident_b[:])
+        mem_sb = const.tile([P, SLOTS // P, D], BF16, name="mem_sb")
+
+        dma_order = []
+        for e in range(len(W_PLAN)):
+            j0 = W_PLAN[e][0]
+            if e == 0:
+                dma_order.append(("a", 0))
+            if e == 2:
+                dma_order.append(("a", 1))
+            if e == 3:
+                dma_order.append(("m", 0))
+            for q in range(2, len(A_PLAN)):
+                if A_PLAN[q][0] - 4 == j0:
+                    dma_order.append(("a", q))
+            dma_order.append(("w", e))
+        issued = [0]
+        w_of = {}
+        a_of = {}
+
+        def issue_through(e_last):
+            while issued[0] < len(dma_order):
+                kind, index = dma_order[issued[0]]
+                if kind == "w" and index > e_last:
+                    break
+                issued[0] += 1
+                if kind == "w":
+                    j0, n = W_PLAN[index]
+                    w_t = wpool.tile([P, GROUP * SLOTS], BF16, name="w_t", tag="w")
+                    nc.sync.dma_start(out=w_t[:, 0 : n * SLOTS], in_=w_rows[:, j0 * SLOTS : (j0 + n) * SLOTS])
+                    for r in range(n):
+                        w_of[j0 + r] = (w_t, r)
+                elif kind == "a":
+                    j0, n = A_PLAN[index]
+                    a_t = const.tile([P, n * D], BF16, name="a_t%d" % index)
+                    nc.sync.dma_start(out=a_t[:], in_=a_rows[:, j0 * D : (j0 + n) * D])
+                    for r in range(n):
+                        a_of[j0 + r] = (a_t, r)
+                else:
+                    nc.sync.dma_start(out=mem_sb[:], in_=m_rows)
+
+        acc = [bank(0, F32), bank(1, F32)]
+        xt_of = {}
+        grouped_of = {}
+        codes = {}
+        scales = {}
+
+        def mm(i, h):
+            w_t, r = w_of[i]
+            a_t, ra = a_of[i]
+            nc.tensor.matmul(
+                out=acc[h][:],
+                lhsT=a_t[:, ra * D : (ra + 1) * D],
+                rhs=w_t[:, r * SLOTS + h * HALF : r * SLOTS + (h + 1) * HALF],
+                start=(i == 0),
+                stop=(i == CHUNKS - 1),
+            )
+
+        def add_memory():
+            for c in range(SLOTS // P):
+                h, cc = divmod(c, HALF // P)
+                nc.tensor.matmul(
+                    out=acc[h][:, cc * P : (cc + 1) * P],
+                    lhsT=mem_sb[:, c, :],
+                    rhs=ident_b[:],
+                    start=False,
+                    stop=False,
+                )
+
+        def transposes(i, quarters):
+            w_t, r = w_of[i]
+            words = w_t[:].bitcast(F32)
+            if i not in xt_of:
+                xt_of[i] = bank(2 + i % 6, F32)
+            for c in quarters:
+                nc.tensor.transpose(
+                    out=xt_of[i][:, c * P : (c + 1) * P],
+                    in_=words[:, r * HALF + c * P : r * HALF + (c + 1) * P],
+                    identity=ident_f[:],
+                )
+
+        def evac(i):
+            k, r = divmod(i, GROUP)
+            if r == 0:
+                grouped_of[k] = gpool.tile([P, GROUP * SLOTS], BF16, name="grouped", tag="grouped", align_bytes=64)
+            dst = grouped_of[k][:].bitcast(F32)[:, r * HALF : (r + 1) * HALF].rearrange("p (g k u) -> p g k u", g=2, u=2)
+            src = xt_of[i][:].rearrange("p (g u k) -> p g k u", g=2, u=2)
+            if r == 0:
+                nc.vector.tensor_copy(out=dst, in_=src)
+            else:
+                nc.scalar.copy(out=dst, in_=src)
+
+        def quant(k):
+            codes[k] = keep.tile([P, GROUP * 2 * P], U32, name="codes%d" % k, align_bytes=64)
+            scales[k] = keep.tile([P, GROUP * 2 * P], U8, name="scales%d" % k, align_bytes=64)
+            nc.vector.quantize_mx(out=codes[k][:].bitcast(FP8X4), scales=scales[k][:], in_=grouped_of[k][:])
+
+        issue_through(AHEAD - 1)
+        entry_at = {}
+        for e in range(len(W_PLAN)):
+            entry_at[W_PLAN[e][0]] = e
+        for i in range(CHUNKS):
+            if i in entry_at:
+                issue_through(entry_at[i] + AHEAD)
+            if i < CHUNKS - LATE:
+                mm(i, 0)
+                transposes(i, [0, 1])
+                mm(i, 1)
+                if i == MEM_AT:
+                    add_memory()
+                transposes(i, [2, 3])
+                evac(i)
+                if i % GROUP == 0 and i >= GROUP:
+                    quant(i // GROUP - 1)
+            else:
+                mm(i, 0)
+                mm(i, 1)
+        quant(GROUPS - 2)
+
+        nm_t = []
+        for h in range(2):
+            nm_t.append(keep.tile([P, HALF], BF16, name="nm_t%d" % h))
+            dst = nm_t[h][:].rearrange("d (u e p) -> d u e p", u=2, e=2)
+            src = acc[h][:].rearrange("d (u p e) -> d u e p", u=2, e=2)
+            if h == 0:
+                nc.vector.tensor_copy(out=dst, in_=src)
+            else:
+                nc.scalar.copy(out=dst, in_=src)
+        transposes(60, [0, 1, 2, 3])
+        transposes(61, [0, 1, 2, 3])
+        nm_p = [bank(6, BF16), bank(7, BF16)]
+        for h in range(2):
+            for t in range(4):
+                nc.tensor.transpose(
+                    out=nm_p[h][:, t * P : (t + 1) * P],
+                    in_=nm_t[h][:, t * P : (t + 1) * P],
+                    identity=ident_b[:],
+                )
+        transposes(62, [0, 1, 2, 3])
+        transposes(63, [0, 1, 2, 3])
+        nm_g = []
+        nm_c = []
+        nm_s = []
+        for h in range(2):
+            nm_g.append(keep.tile([P, HALF], BF16, name="nm_g%d" % h, align_bytes=64))
+            nm_c.append(keep.tile([P, P], U32, name="nm_c%d" % h, align_bytes=64))
+            nm_s.append(keep.tile([P, P], U8, name="nm_s%d" % h, align_bytes=64))
+            dst = nm_g[h][:].rearrange("p (d t) -> p d t", t=4)
+            src = nm_p[h][:].rearrange("p (t d) -> p d t", t=4)
+            if h == 0:
+                nc.scalar.copy(out=dst, in_=src)
+            else:
+                nc.vector.tensor_copy(out=dst, in_=src)
+        for h in range(2):
+            nc.vector.quantize_mx(out=nm_c[h][:].bitcast(FP8X4), scales=nm_s[h][:], in_=nm_g[h][:])
+        for i in range(CHUNKS - LATE, CHUNKS):
+            evac(i)
+
+        for b in range(GROUPS):
+            r_t = bank(R_BANKS[b % 8], F32)
+            for jj in range(GROUP):
+                for g in range(2):
+                    col = (jj * 2 + g) * P
+                    nc.tensor.matmul_mx(
+                        out=r_t[:, jj * P : (jj + 1) * P],
+                        lhsT=codes[b][:, col : col + P].bitcast(FP8X4),
+                        lhsT_scale=scales[b][:, col : col + P],
+                        rhs=nm_c[g][:].bitcast(FP8X4),
+                        rhs_scale=nm_s[g][:],
+                        start=(g == 0),
+                        stop=(g == 1),
+                    )
+            o_t = opool.tile([P, HALF], F32, name="o_t", tag="o")
+            if b in R_ON_VECTOR:
+                nc.vector.tensor_copy(out=o_t[:], in_=r_t[:])
+            else:
+                nc.scalar.copy(out=o_t[:], in_=r_t[:])
+            nc.sync.dma_start(out=o_rows[:, b * HALF : (b + 1) * HALF], in_=o_t[:])
+            if b == 0:
+                quant(GROUPS - 1)

@@ -19,9 +19,10 @@ GROUP = 4
 GROUPS = CHUNKS // GROUP
 FLOPS = 2 * 2 * KEYS * SLOTS * D
 
-W_PLAN = [(0, 1), (1, 1), (2, 2)] + [(j, 4) for j in range(4, 60, 4)] + [(60, 1), (61, 1), (62, 1), (63, 1)]
-A_PLAN = [(0, 4), (4, 12), (16, 16), (32, 16), (48, 16)]
-W_BUFS = 8
+W_PLAN = [(0, 1), (1, 1), (2, 2), (4, 4)] + [(j, 8) for j in range(8, 56, 8)] + [(56, 4), (60, 2), (62, 1), (63, 1)]
+W_MAX = 8
+A_PLAN = [(0, 4), (4, 4)] + [(j, 8) for j in range(8, 64, 8)]
+W_BUFS = 5
 AHEAD = W_BUFS - 1
 MEM_AT = 6
 LATE = 4
@@ -57,15 +58,11 @@ def tile_memory_pb_t_kernel(tc, w, memory, add, out):
         dma_order = []
         for e in range(len(W_PLAN)):
             j0 = W_PLAN[e][0]
-            if e == 0:
-                dma_order.append(("a", 0))
-            if e == 2:
-                dma_order.append(("a", 1))
-            if e == 3:
-                dma_order.append(("m", 0))
-            for q in range(2, len(A_PLAN)):
-                if A_PLAN[q][0] - 4 == j0:
+            for q in range(len(A_PLAN)):
+                if A_PLAN[q][0] == j0:
                     dma_order.append(("a", q))
+            if j0 == 4:
+                dma_order.append(("m", 0))
             dma_order.append(("w", e))
         issued = [0]
         w_of = {}
@@ -79,7 +76,7 @@ def tile_memory_pb_t_kernel(tc, w, memory, add, out):
                 issued[0] += 1
                 if kind == "w":
                     j0, n = W_PLAN[index]
-                    w_t = wpool.tile([P, GROUP * SLOTS], BF16, name="w_t", tag="w")
+                    w_t = wpool.tile([P, W_MAX * SLOTS], BF16, name="w_t", tag="w")
                     nc.sync.dma_start(out=w_t[:, 0 : n * SLOTS], in_=w_rows[:, j0 * SLOTS : (j0 + n) * SLOTS])
                     for r in range(n):
                         w_of[j0 + r] = (w_t, r)

@@ -19,15 +19,20 @@ GROUP = 4
 GROUPS = CHUNKS // GROUP
 FLOPS = 2 * 2 * KEYS * SLOTS * D
 
-W_PLAN = [(0, 1), (1, 1), (2, 2), (4, 4)] + [(j, 8) for j in range(8, 56, 8)] + [(56, 4), (60, 2), (62, 1), (63, 1)]
-W_MAX = 8
+W_SIZES = [1, 1, 2] + [4] * 11 + [2] * 6 + [1] * 4
+W_PLAN = [(sum(W_SIZES[:e]), W_SIZES[e]) for e in range(len(W_SIZES))]
+W_MAX = 4
 A_PLAN = [(0, 4), (4, 4)] + [(j, 8) for j in range(8, 64, 8)]
-W_BUFS = 5
+M_PLAN = [(0, 4), (4, 4)]
+W_BUFS = 8
 AHEAD = W_BUFS - 1
-MEM_AT = 6
 LATE = 4
+R_SIZES = [4] * 16
+R_PLAN = [(sum(R_SIZES[:b]), R_SIZES[b]) for b in range(len(R_SIZES))]
+LAST_QUANT_AFTER = 0
+O_BUFS = 12
 R_BANKS = [0, 1, 6, 7, 2, 3, 4, 5]
-R_ON_VECTOR = [0, 3, 5, 7, 9, 11, 13, 15]
+R_ON_VECTOR = [0, 3, 5, 7, 9, 11, 13, 15, 17]
 
 
 def tile_memory_pb_t_kernel(tc, w, memory, add, out):
@@ -42,7 +47,7 @@ def tile_memory_pb_t_kernel(tc, w, memory, add, out):
         keep = ctx.enter_context(tc.tile_pool(name="keep", bufs=1))
         wpool = ctx.enter_context(tc.tile_pool(name="wpool", bufs=W_BUFS))
         gpool = ctx.enter_context(tc.tile_pool(name="gpool", bufs=3))
-        opool = ctx.enter_context(tc.tile_pool(name="opool", bufs=6))
+        opool = ctx.enter_context(tc.tile_pool(name="opool", bufs=O_BUFS))
         psum = ctx.enter_context(tc.psum_pool(name="psum", bufs=1))
         ctx.enter_context(tc.manual_schedule())
 
@@ -53,7 +58,6 @@ def tile_memory_pb_t_kernel(tc, w, memory, add, out):
         make_identity(nc, ident_f[:])
         ident_b = const.tile([P, P], BF16, name="ident_b")
         make_identity(nc, ident_b[:])
-        mem_sb = const.tile([P, SLOTS // P, D], BF16, name="mem_sb")
 
         dma_order = []
         for e in range(len(W_PLAN)):
@@ -61,12 +65,13 @@ def tile_memory_pb_t_kernel(tc, w, memory, add, out):
             for q in range(len(A_PLAN)):
                 if A_PLAN[q][0] == j0:
                     dma_order.append(("a", q))
-            if j0 == 4:
-                dma_order.append(("m", 0))
             dma_order.append(("w", e))
+        for q in range(len(M_PLAN)):
+            dma_order.append(("m", q))
         issued = [0]
         w_of = {}
         a_of = {}
+        m_of = {}
 
         def issue_through(e_last):
             while issued[0] < len(dma_order):
@@ -87,7 +92,11 @@ def tile_memory_pb_t_kernel(tc, w, memory, add, out):
                     for r in range(n):
                         a_of[j0 + r] = (a_t, r)
                 else:
-                    nc.sync.dma_start(out=mem_sb[:], in_=m_rows)
+                    c0, n = M_PLAN[index]
+                    m_t = const.tile([P, n, D], BF16, name="m_t%d" % index)
+                    nc.sync.dma_start(out=m_t[:], in_=m_rows[:, c0 : c0 + n, :])
+                    for r in range(n):
+                        m_of[c0 + r] = (m_t, r)
 
         acc = [bank(0, F32), bank(1, F32)]
         xt_of = {}
@@ -103,18 +112,19 @@ def tile_memory_pb_t_kernel(tc, w, memory, add, out):
                 lhsT=a_t[:, ra * D : (ra + 1) * D],
                 rhs=w_t[:, r * SLOTS + h * HALF : r * SLOTS + (h + 1) * HALF],
                 start=(i == 0),
-                stop=(i == CHUNKS - 1),
+                stop=False,
             )
 
         def add_memory():
             for c in range(SLOTS // P):
                 h, cc = divmod(c, HALF // P)
+                m_t, r = m_of[c]
                 nc.tensor.matmul(
                     out=acc[h][:, cc * P : (cc + 1) * P],
-                    lhsT=mem_sb[:, c, :],
+                    lhsT=m_t[:, r, :],
                     rhs=ident_b[:],
                     start=False,
-                    stop=False,
+                    stop=(cc == HALF // P - 1),
                 )
 
         def transposes(i, quarters):
@@ -156,8 +166,6 @@ def tile_memory_pb_t_kernel(tc, w, memory, add, out):
                 mm(i, 0)
                 transposes(i, [0, 1])
                 mm(i, 1)
-                if i == MEM_AT:
-                    add_memory()
                 transposes(i, [2, 3])
                 evac(i)
                 if i % GROUP == 0 and i >= GROUP:
@@ -165,6 +173,7 @@ def tile_memory_pb_t_kernel(tc, w, memory, add, out):
             else:
                 mm(i, 0)
                 mm(i, 1)
+        add_memory()
         quant(GROUPS - 2)
 
         nm_t = []
@@ -206,15 +215,17 @@ def tile_memory_pb_t_kernel(tc, w, memory, add, out):
         for i in range(CHUNKS - LATE, CHUNKS):
             evac(i)
 
-        for b in range(GROUPS):
+        for b in range(len(R_PLAN)):
+            c0, n = R_PLAN[b]
             r_t = bank(R_BANKS[b % 8], F32)
-            for jj in range(GROUP):
+            for jj in range(n):
+                k, r = divmod(c0 + jj, GROUP)
                 for g in range(2):
-                    col = (jj * 2 + g) * P
+                    col = (r * 2 + g) * P
                     nc.tensor.matmul_mx(
                         out=r_t[:, jj * P : (jj + 1) * P],
-                        lhsT=codes[b][:, col : col + P].bitcast(FP8X4),
-                        lhsT_scale=scales[b][:, col : col + P],
+                        lhsT=codes[k][:, col : col + P].bitcast(FP8X4),
+                        lhsT_scale=scales[k][:, col : col + P],
                         rhs=nm_c[g][:].bitcast(FP8X4),
                         rhs_scale=nm_s[g][:],
                         start=(g == 0),
@@ -222,9 +233,9 @@ def tile_memory_pb_t_kernel(tc, w, memory, add, out):
                     )
             o_t = opool.tile([P, HALF], F32, name="o_t", tag="o")
             if b in R_ON_VECTOR:
-                nc.vector.tensor_copy(out=o_t[:], in_=r_t[:])
+                nc.vector.tensor_copy(out=o_t[:, 0 : n * D], in_=r_t[:, 0 : n * D])
             else:
-                nc.scalar.copy(out=o_t[:], in_=r_t[:])
-            nc.sync.dma_start(out=o_rows[:, b * HALF : (b + 1) * HALF], in_=o_t[:])
-            if b == 0:
+                nc.scalar.copy(out=o_t[:, 0 : n * D], in_=r_t[:, 0 : n * D])
+            nc.sync.dma_start(out=o_rows[:, c0 * D : (c0 + n) * D], in_=o_t[:, 0 : n * D])
+            if b == LAST_QUANT_AFTER:
                 quant(GROUPS - 1)

@@ -31,6 +31,8 @@ R_SIZES = [4] * 16
 R_PLAN = [(sum(R_SIZES[:b]), R_SIZES[b]) for b in range(len(R_SIZES))]
 LAST_QUANT_AFTER = 0
 O_BUFS = 12
+DUMMIES_A = 2
+DUMMIES_B = 1
 R_BANKS = [0, 1, 6, 7, 2, 3, 4, 5]
 R_ON_VECTOR = [0, 3, 5, 7, 9, 11, 13, 15, 17]
 
@@ -155,6 +157,12 @@ def tile_memory_pb_t_kernel(tc, w, memory, add, out):
             scales[k] = keep.tile([P, GROUP * 2 * P], U8, name="scales%d" % k, align_bytes=64)
             nc.vector.quantize_mx(out=codes[k][:].bitcast(FP8X4), scales=scales[k][:], in_=grouped_of[k][:])
 
+        def dummies(index, count):
+            if count > 0:
+                d_t = bank(index, F32)
+                for q in range(count):
+                    nc.tensor.matmul(out=d_t[:], lhsT=ident_b[:], rhs=a_of[0][0][:], start=True, stop=True)
+
         issue_through(AHEAD - 1)
         entry_at = {}
         for e in range(len(W_PLAN)):
@@ -185,8 +193,7 @@ def tile_memory_pb_t_kernel(tc, w, memory, add, out):
                 nc.vector.tensor_copy(out=dst, in_=src)
             else:
                 nc.scalar.copy(out=dst, in_=src)
-        transposes(60, [0, 1, 2, 3])
-        transposes(61, [0, 1, 2, 3])
+        dummies(2, DUMMIES_A)
         nm_p = [bank(6, BF16), bank(7, BF16)]
         for h in range(2):
             for t in range(4):
@@ -195,8 +202,9 @@ def tile_memory_pb_t_kernel(tc, w, memory, add, out):
                     in_=nm_t[h][:, t * P : (t + 1) * P],
                     identity=ident_b[:],
                 )
-        transposes(62, [0, 1, 2, 3])
-        transposes(63, [0, 1, 2, 3])
+        for i in range(CHUNKS - LATE, CHUNKS):
+            transposes(i, [0, 1, 2, 3])
+        dummies(1, DUMMIES_B)
         nm_g = []
         nm_c = []
         nm_s = []

@@ -26,13 +26,13 @@ A_PLAN = [(0, 4), (4, 4)] + [(j, 8) for j in range(8, 64, 8)]
 M_PLAN = [(0, 4), (4, 4)]
 W_BUFS = 8
 AHEAD = W_BUFS - 1
-LATE = 4
+LATE = 2
 R_SIZES = [4] * 16
 R_PLAN = [(sum(R_SIZES[:b]), R_SIZES[b]) for b in range(len(R_SIZES))]
 LAST_QUANT_AFTER = 0
 O_BUFS = 12
 DUMMIES_A = 2
-DUMMIES_B = 1
+DUMMIES_B = 2
 R_BANKS = [0, 1, 6, 7, 2, 3, 4, 5]
 R_ON_VECTOR = [0, 3, 5, 7, 9, 11, 13, 15, 17]
 
@@ -182,7 +182,8 @@ def tile_memory_pb_t_kernel(tc, w, memory, add, out):
                 mm(i, 0)
                 mm(i, 1)
         add_memory()
-        quant(GROUPS - 2)
+        if LATE >= GROUP:
+            quant(GROUPS - 2)
 
         nm_t = []
         for h in range(2):

from contextlib import ExitStack

import concourse.mybir as mybir
from concourse.masks import make_identity

F32 = mybir.dt.float32
BF16 = mybir.dt.bfloat16
U32 = mybir.dt.uint32
U8 = mybir.dt.uint8
FP8X4 = mybir.dt.float8_e4m3fn_x4

P = 128
KEYS = 8192
SLOTS = 1024
D = 128
CHUNKS = KEYS // P
HALF = 512
GROUP = 4
GROUPS = CHUNKS // GROUP
FLOPS = 2 * 2 * KEYS * SLOTS * D

W_SIZES = [1, 1, 2] + [4] * 11 + [2] * 6 + [1] * 4
W_PLAN = [(sum(W_SIZES[:e]), W_SIZES[e]) for e in range(len(W_SIZES))]
W_MAX = 4
A_PLAN = [(0, 4), (4, 4)] + [(j, 8) for j in range(8, 64, 8)]
M_PLAN = [(0, 4), (4, 4)]
W_BUFS = 8
AHEAD = W_BUFS - 1
LATE = 2
R_SIZES = [4] * 16
R_PLAN = [(sum(R_SIZES[:b]), R_SIZES[b]) for b in range(len(R_SIZES))]
LAST_QUANT_AFTER = 0
O_BUFS = 12
DUMMIES_A = 2
DUMMIES_B = 2
R_BANKS = [0, 1, 6, 7, 2, 3, 4, 5]
R_ON_VECTOR = [0, 3, 5, 7, 9, 11, 13, 15, 17]


def tile_memory_pb_t_kernel(tc, w, memory, add, out):
    nc = tc.nc
    w_rows = w.rearrange("(p j) n -> p (j n)", j=CHUNKS)
    a_rows = add.rearrange("(p j) c h w -> p (j c h w)", j=CHUNKS)
    o_rows = out.rearrange("(p j) c h w -> p (j c h w)", j=CHUNKS)
    m_rows = memory.rearrange("(c p) a h w -> p c (a h w)", p=P)

    with ExitStack() as ctx:
        const = ctx.enter_context(tc.tile_pool(name="const", bufs=1))
        keep = ctx.enter_context(tc.tile_pool(name="keep", bufs=1))
        wpool = ctx.enter_context(tc.tile_pool(name="wpool", bufs=W_BUFS))
        gpool = ctx.enter_context(tc.tile_pool(name="gpool", bufs=3))
        opool = ctx.enter_context(tc.tile_pool(name="opool", bufs=O_BUFS))
        psum = ctx.enter_context(tc.psum_pool(name="psum", bufs=1))
        ctx.enter_context(tc.manual_schedule())

        def bank(index, dtype):
            return psum.tile([P, HALF], dtype, name="ps%d" % index, tag="b%d" % index)

        ident_f = const.tile([P, P], F32, name="ident_f")
        make_identity(nc, ident_f[:])
        ident_b = const.tile([P, P], BF16, name="ident_b")
        make_identity(nc, ident_b[:])

        dma_order = []
        for e in range(len(W_PLAN)):
            j0 = W_PLAN[e][0]
            for q in range(len(A_PLAN)):
                if A_PLAN[q][0] == j0:
                    dma_order.append(("a", q))
            dma_order.append(("w", e))
        for q in range(len(M_PLAN)):
            dma_order.append(("m", q))
        issued = [0]
        w_of = {}
        a_of = {}
        m_of = {}

        def issue_through(e_last):
            while issued[0] < len(dma_order):
                kind, index = dma_order[issued[0]]
                if kind == "w" and index > e_last:
                    break
                issued[0] += 1
                if kind == "w":
                    j0, n = W_PLAN[index]
                    w_t = wpool.tile([P, W_MAX * SLOTS], BF16, name="w_t", tag="w")
                    nc.sync.dma_start(out=w_t[:, 0 : n * SLOTS], in_=w_rows[:, j0 * SLOTS : (j0 + n) * SLOTS])
                    for r in range(n):
                        w_of[j0 + r] = (w_t, r)
                elif kind == "a":
                    j0, n = A_PLAN[index]
                    a_t = const.tile([P, n * D], BF16, name="a_t%d" % index)
                    nc.sync.dma_start(out=a_t[:], in_=a_rows[:, j0 * D : (j0 + n) * D])
                    for r in range(n):
                        a_of[j0 + r] = (a_t, r)
                else:
                    c0, n = M_PLAN[index]
                    m_t = const.tile([P, n, D], BF16, name="m_t%d" % index)
                    nc.sync.dma_start(out=m_t[:], in_=m_rows[:, c0 : c0 + n, :])
                    for r in range(n):
                        m_of[c0 + r] = (m_t, r)

        acc = [bank(0, F32), bank(1, F32)]
        xt_of = {}
        grouped_of = {}
        codes = {}
        scales = {}

        def mm(i, h):
            w_t, r = w_of[i]
            a_t, ra = a_of[i]
            nc.tensor.matmul(
                out=acc[h][:],
                lhsT=a_t[:, ra * D : (ra + 1) * D],
                rhs=w_t[:, r * SLOTS + h * HALF : r * SLOTS + (h + 1) * HALF],
                start=(i == 0),
                stop=False,
            )

        def add_memory():
            for c in range(SLOTS // P):
                h, cc = divmod(c, HALF // P)
                m_t, r = m_of[c]
                nc.tensor.matmul(
                    out=acc[h][:, cc * P : (cc + 1) * P],
                    lhsT=m_t[:, r, :],
                    rhs=ident_b[:],
                    start=False,
                    stop=(cc == HALF // P - 1),
                )

        def transposes(i, quarters):
            w_t, r = w_of[i]
            words = w_t[:].bitcast(F32)
            if i not in xt_of:
                xt_of[i] = bank(2 + i % 6, F32)
            for c in quarters:
                nc.tensor.transpose(
                    out=xt_of[i][:, c * P : (c + 1) * P],
                    in_=words[:, r * HALF + c * P : r * HALF + (c + 1) * P],
                    identity=ident_f[:],
                )

        def evac(i):
            k, r = divmod(i, GROUP)
            if r == 0:
                grouped_of[k] = gpool.tile([P, GROUP * SLOTS], BF16, name="grouped", tag="grouped", align_bytes=64)
            dst = grouped_of[k][:].bitcast(F32)[:, r * HALF : (r + 1) * HALF].rearrange("p (g k u) -> p g k u", g=2, u=2)
            src = xt_of[i][:].rearrange("p (g u k) -> p g k u", g=2, u=2)
            if r == 0:
                nc.vector.tensor_copy(out=dst, in_=src)
            else:
                nc.scalar.copy(out=dst, in_=src)

        def quant(k):
            codes[k] = keep.tile([P, GROUP * 2 * P], U32, name="codes%d" % k, align_bytes=64)
            scales[k] = keep.tile([P, GROUP * 2 * P], U8, name="scales%d" % k, align_bytes=64)
            nc.vector.quantize_mx(out=codes[k][:].bitcast(FP8X4), scales=scales[k][:], in_=grouped_of[k][:])

        def dummies(index, count):
            if count > 0:
                d_t = bank(index, F32)
                for q in range(count):
                    nc.tensor.matmul(out=d_t[:], lhsT=ident_b[:], rhs=a_of[0][0][:], start=True, stop=True)

        issue_through(AHEAD - 1)
        entry_at = {}
        for e in range(len(W_PLAN)):
            entry_at[W_PLAN[e][0]] = e
        for i in range(CHUNKS):
            if i in entry_at:
                issue_through(entry_at[i] + AHEAD)
            if i < CHUNKS - LATE:
                mm(i, 0)
                transposes(i, [0, 1])
                mm(i, 1)
                transposes(i, [2, 3])
                evac(i)
                if i % GROUP == 0 and i >= GROUP:
                    quant(i // GROUP - 1)
            else:
                mm(i, 0)
                mm(i, 1)
        add_memory()
        if LATE >= GROUP:
            quant(GROUPS - 2)

        nm_t = []
        for h in range(2):
            nm_t.append(keep.tile([P, HALF], BF16, name="nm_t%d" % h))
            dst = nm_t[h][:].rearrange("d (u e p) -> d u e p", u=2, e=2)
            src = acc[h][:].rearrange("d (u p e) -> d u e p", u=2, e=2)
            if h == 0:
                nc.vector.tensor_copy(out=dst, in_=src)
            else:
                nc.scalar.copy(out=dst, in_=src)
        dummies(2, DUMMIES_A)
        nm_p = [bank(6, BF16), bank(7, BF16)]
        for h in range(2):
            for t in range(4):
                nc.tensor.transpose(
                    out=nm_p[h][:, t * P : (t + 1) * P],
                    in_=nm_t[h][:, t * P : (t + 1) * P],
                    identity=ident_b[:],
                )
        for i in range(CHUNKS - LATE, CHUNKS):
            transposes(i, [0, 1, 2, 3])
        dummies(1, DUMMIES_B)
        nm_g = []
        nm_c = []
        nm_s = []
        for h in range(2):
            nm_g.append(keep.tile([P, HALF], BF16, name="nm_g%d" % h, align_bytes=64))
            nm_c.append(keep.tile([P, P], U32, name="nm_c%d" % h, align_bytes=64))
            nm_s.append(keep.tile([P, P], U8, name="nm_s%d" % h, align_bytes=64))
            dst = nm_g[h][:].rearrange("p (d t) -> p d t", t=4)
            src = nm_p[h][:].rearrange("p (t d) -> p d t", t=4)
            if h == 0:
                nc.scalar.copy(out=dst, in_=src)
            else:
                nc.vector.tensor_copy(out=dst, in_=src)
        for h in range(2):
            nc.vector.quantize_mx(out=nm_c[h][:].bitcast(FP8X4), scales=nm_s[h][:], in_=nm_g[h][:])
        for i in range(CHUNKS - LATE, CHUNKS):
            evac(i)

        for b in range(len(R_PLAN)):
            c0, n = R_PLAN[b]
            r_t = bank(R_BANKS[b % 8], F32)
            for jj in range(n):
                k, r = divmod(c0 + jj, GROUP)
                for g in range(2):
                    col = (r * 2 + g) * P
                    nc.tensor.matmul_mx(
                        out=r_t[:, jj * P : (jj + 1) * P],
                        lhsT=codes[k][:, col : col + P].bitcast(FP8X4),
                        lhsT_scale=scales[k][:, col : col + P],
                        rhs=nm_c[g][:].bitcast(FP8X4),
                        rhs_scale=nm_s[g][:],
                        start=(g == 0),
                        stop=(g == 1),
                    )
            o_t = opool.tile([P, HALF], F32, name="o_t", tag="o")
            if b in R_ON_VECTOR:
                nc.vector.tensor_copy(out=o_t[:, 0 : n * D], in_=r_t[:, 0 : n * D])
            else:
                nc.scalar.copy(out=o_t[:, 0 : n * D], in_=r_t[:, 0 : n * D])
            nc.sync.dma_start(out=o_rows[:, c0 * D : (c0 + n) * D], in_=o_t[:, 0 : n * D])
            if b == LAST_QUANT_AFTER:
                quant(GROUPS - 1)
